import numpy as np
import ml_dtypes


def mxq(x, axis, fmt="e4m3"):
    dtype, down = {"e4m3": (ml_dtypes.float8_e4m3fn, 7), "e5m2": (ml_dtypes.float8_e5m2, 14)}[fmt]
    v = np.moveaxis(np.asarray(x, np.float32).astype(ml_dtypes.bfloat16).astype(np.float64), axis, -1)
    blocks = v.reshape(v.shape[:-1] + (-1, 32))
    amax = np.abs(blocks).max(-1, keepdims=True)
    byte = np.maximum(np.where(amax > 0, np.frexp(amax)[1] - 1 + 127, 0) - down, 1)
    scale = np.exp2(byte - 127.0)
    codes = (blocks / scale).astype(np.float32).astype(dtype).astype(np.float64)
    return np.moveaxis((codes * scale).reshape(v.shape), -1, axis)


WIDE = False


def mx_kscale(k):
    if not WIDE:
        return np.ones(k)
    levels = np.array([10, -10, 5, -5, 0])
    a = np.random.permutation(np.resize(levels, k // 512 * 4)).reshape(k // 512, 4)
    idx = np.arange(k)
    return np.exp2(a[idx // 512, idx % 128 // 32])


BF16 = ml_dtypes.bfloat16


def bf(x):
    return np.asarray(x, np.float32).astype(BF16)


def f64(x):
    return np.asarray(x).astype(np.float64)


H, D, L = 4, 1024, 512
HD = H * D


def split_heads(x):
    return x.reshape(L, H, D).transpose(1, 2, 0)


def setup_inputs():
    s = mx_kscale(D)
    return {"tokens": bf(np.random.standard_normal((D, L)) * s[:, None]),
            "Wq": bf(np.random.standard_normal((HD, D)) / np.sqrt(D) / s),
            "bq": bf(np.random.standard_normal(HD) * 0.2),
            "Wk": bf(np.random.standard_normal((HD, D)) / np.sqrt(D) / s),
            "bk": bf(np.random.standard_normal(HD) * 0.2)}


def reference(tokens, Wq, bq, Wk, bk):
    tq = mxq(f64(tokens), 0, "e4m3")
    q = split_heads((mxq(f64(Wq), 1, "e4m3") @ tq) + f64(bq)[:, None])
    k = split_heads((mxq(f64(Wk), 1, "e4m3") @ tq) + f64(bk)[:, None])
    scores = (mxq(q.transpose(0, 2, 1), 2, "e4m3") @ mxq(k, 1, "e4m3")) / np.sqrt(D)
    e = np.exp(scores - scores.max(0, keepdims=True))
    return e / e.sum(0, keepdims=True)

@@ -1,0 +1,227 @@
+from contextlib import ExitStack
+
+import concourse.mybir as mybir
+from concourse.masks import make_identity
+
+F32 = mybir.dt.float32
+BF16 = mybir.dt.bfloat16
+U32 = mybir.dt.uint32
+U8 = mybir.dt.uint8
+FP8X4 = mybir.dt.float8_e4m3fn_x4
+ALU = mybir.AluOpType
+ACT = mybir.ActivationFunctionType
+AX = mybir.AxisListType
+
+P = 128
+H = 4
+L = 512
+D = 1024
+NCH = 4
+UNITS = 2 * NCH * H
+W_BUFS = 8
+AHEAD = 2
+
+FLOPS = 2 * (2 * H * D) * D * L + 2 * H * L * L * D
+
+
+def tile_selfattention_pa_kernel(tc, tokens, Wq, bq, Wk, bk, out):
+    nc = tc.nc
+    with ExitStack() as ctx:
+        const = ctx.enter_context(tc.tile_pool(name="const", bufs=1))
+        wraw_pool = ctx.enter_context(tc.tile_pool(name="wraw", bufs=W_BUFS))
+        stage = ctx.enter_context(tc.tile_pool(name="stage", bufs=3))
+        soft = ctx.enter_context(tc.tile_pool(name="soft", bufs=2))
+        ps_t = ctx.enter_context(tc.psum_pool(name="ps_t", bufs=2))
+        ps_m = ctx.enter_context(tc.psum_pool(name="ps_m", bufs=4))
+        ps_s = ctx.enter_context(tc.psum_pool(name="ps_s", bufs=2))
+        ctx.enter_context(tc.manual_schedule())
+
+        w_src = {"k": Wk.rearrange("(i l h e) k -> i h l (e k)", i=NCH, l=P, h=H, e=2),
+                 "q": Wq.rearrange("(i l h e) k -> i h l (e k)", i=NCH, l=P, h=H, e=2)}
+        out_v = out.rearrange("h (i p) (j m) -> i j p h m", p=P, m=P)
+
+        def unit(u):
+            return ("k" if u < NCH * H else "q"), (u // H) % NCH, u % H
+
+        ident = const.tile([P, P], F32, name="ident")
+        make_identity(nc, ident[:])
+        tok_raw = const.tile([P, 2, 4, L], BF16, name="tok_raw")
+        tok_grp = const.tile([P, 2, L, 4], BF16, name="tok_grp", align_bytes=64)
+        tok_codes = const.tile([P, 2, L], U32, name="tok_codes", align_bytes=64)
+        tok_scl = const.tile([P, 2, L], U8, name="tok_scl", align_bytes=64)
+        bias = {"k": const.tile([P, H * D], BF16, name="bias_k"), "q": const.tile([P, H * D], BF16, name="bias_q")}
+        codes = {"k": const.tile([P, NCH, H, 2, P], U32, name="k_codes", align_bytes=64),
+                 "q": const.tile([P, NCH, H, 2, P], U32, name="q_codes", align_bytes=64)}
+        scl = {"k": const.tile([P, NCH, H, 2, P], U8, name="k_scl", align_bytes=64),
+               "q": const.tile([P, NCH, H, 2, P], U8, name="q_scl", align_bytes=64)}
+
+        w_raw = {}
+        wt_grp = {}
+        w_codes = {}
+        w_scl = {}
+        qk_grp = {}
+        banks_m = {}
+
+        def load(u):
+            which, i, h = unit(u)
+            w_raw[u] = wraw_pool.tile([P, 2, D], BF16, name="w_raw")
+            nc.sync.dma_start(out=w_raw[u][:].rearrange("p e k -> p (e k)"), in_=w_src[which][i, h])
+
+        def transposes(u):
+            w32 = w_raw[u][:].bitcast(F32)
+            wt_grp[u] = stage.tile([P, 2, 4 * 2 * P], BF16, name="wt_grp", align_bytes=64)
+            for g in range(2):
+                bank = ps_t.tile([P, 4 * P], F32, name="bank_t")
+                for e in range(2):
+                    for v in range(2):
+                        nc.tensor.transpose(out=bank[:, (2 * e + v) * P:(2 * e + v + 1) * P],
+                                            in_=w32[:, e, 256 * g + P * v:256 * g + P * (v + 1)], identity=ident[:])
+                nc.scalar.copy(out=wt_grp[u][:, g, :].bitcast(F32).rearrange("p (e l v) -> p e l v", e=2, v=2),
+                               in_=bank[:].rearrange("p (e v l) -> p e l v", e=2, v=2))
+
+        def quant_w(u):
+            w_codes[u] = stage.tile([P, 2, 2 * P], U32, name="w_codes", align_bytes=64)
+            w_scl[u] = stage.tile([P, 2, 2 * P], U8, name="w_scl", align_bytes=64)
+            nc.vector.quantize_mx(out=w_codes[u][:].rearrange("p g c -> p (g c)").bitcast(FP8X4),
+                                  scales=w_scl[u][:].rearrange("p g c -> p (g c)"),
+                                  in_=wt_grp[u][:].rearrange("p g x -> p (g x)"))
+
+        def products(u):
+            banks_m[u] = []
+            for a in range(2):
+                bank = ps_m.tile([P, 4 * P], F32, name="bank_m")
+                banks_m[u].append(bank)
+                for b in range(2):
+                    cb = 2 * a + b
+                    for g in range(2):
+                        nc.tensor.matmul_mx(out=bank[:, 2 * P * b:2 * P * (b + 1)],
+                                            lhsT=tok_codes[:, g, P * cb:P * (cb + 1)].bitcast(FP8X4),
+                                            lhsT_scale=tok_scl[:, g, P * cb:P * (cb + 1)],
+                                            rhs=w_codes[u][:, g, :].bitcast(FP8X4), rhs_scale=w_scl[u][:, g, :],
+                                            start=(g == 0), stop=(g == 1))
+
+        def add_bias(u):
+            which, i, h = unit(u)
+            qk_grp[u] = stage.tile([P, 2, P, 2, 2], BF16, name="qk_grp", align_bytes=64)
+            b_v = bias[which][:].rearrange("p (i l h e) -> p i h l e", i=NCH, l=P, h=H, e=2)[:, i, h]
+            for a in range(2):
+                nc.vector.tensor_tensor(out=qk_grp[u][:, a],
+                                        in0=banks_m[u][a][:].rearrange("p (b e l) -> p l b e", b=2, e=2),
+                                        in1=b_v.unsqueeze(2).to_broadcast([P, P, 2, 2]), op=ALU.add)
+
+        def quant_qk(u):
+            which, i, h = unit(u)
+            nc.vector.quantize_mx(out=codes[which][:, i, h].rearrange("p a l -> p (a l)").bitcast(FP8X4),
+                                  scales=scl[which][:, i, h].rearrange("p a l -> p (a l)"),
+                                  in_=qk_grp[u][:].rearrange("p a l b e -> p (a l b e)"))
+
+        bank_s = {}
+        e_t = {}
+        sums = {}
+        rinv = {}
+
+        def scores(i, j):
+            bank_s[i, j] = ps_s.tile([P, H, P], F32, name="bank_s")
+            for h in range(H):
+                for a in range(2):
+                    nc.tensor.matmul_mx(out=bank_s[i, j][:, h, :],
+                                        lhsT=codes["q"][:, i, h, a, :].bitcast(FP8X4), lhsT_scale=scl["q"][:, i, h, a, :],
+                                        rhs=codes["k"][:, j, h, a, :].bitcast(FP8X4), rhs_scale=scl["k"][:, j, h, a, :],
+                                        start=(a == 0), stop=(a == 1))
+
+        def shift(i, j):
+            mx = soft.tile([P, P], F32, name="mx")
+            nc.vector.tensor_reduce(out=mx[:], in_=bank_s[i, j][:].rearrange("p h m -> p m h"), axis=AX.X, op=ALU.max)
+            e_t[i, j] = soft.tile([P, H, P], F32, name="e_t", bufs=12)
+            nc.vector.tensor_tensor(out=e_t[i, j][:], in0=bank_s[i, j][:],
+                                    in1=mx[:].unsqueeze(1).to_broadcast([P, H, P]), op=ALU.subtract)
+
+        def expo(i, j):
+            nc.scalar.activation(out=e_t[i, j][:], in_=e_t[i, j][:], func=ACT.Exp, scale=1.0 / 32.0)
+
+        def total(i, j):
+            if j == 0:
+                sums[i] = soft.tile([P, NCH, P], F32, name="sums", bufs=3)
+                rinv[i] = soft.tile([P, NCH, P], F32, name="rinv", bufs=3)
+            half = soft.tile([P, 2, P], F32, name="half")
+            nc.gpsimd.tensor_tensor(out=half[:], in0=e_t[i, j][:, 0:2, :], in1=e_t[i, j][:, 2:4, :], op=ALU.add)
+            nc.gpsimd.tensor_tensor(out=sums[i][:, j, :], in0=half[:, 0, :], in1=half[:, 1, :], op=ALU.add)
+
+        def invert(i):
+            lns = soft.tile([P, NCH, P], F32, name="lns")
+            nc.scalar.activation(out=lns[:], in_=sums[i][:], func=ACT.Ln)
+            nc.scalar.activation(out=rinv[i][:], in_=lns[:], func=ACT.Exp, scale=-1.0)
+
+        def scale_block(i, j, eng):
+            eng.tensor_tensor(out=e_t[i, j][:], in0=e_t[i, j][:],
+                              in1=rinv[i][:, j, :].unsqueeze(1).to_broadcast([P, H, P]), op=ALU.mult)
+            nc.sync.dma_start(out=out_v[i, j], in_=e_t[i, j][:])
+
+        tok_src = tokens.rearrange("(g v p e) c -> g p v (e c)", g=2, v=2, p=P, e=2)
+        for g in range(2):
+            nc.sync.dma_start(out=tok_raw[:, g].rearrange("p (v e) c -> p v (e c)", v=2), in_=tok_src[g])
+        for u in range(3):
+            load(u)
+        nc.sync.dma_start(out=bias["k"][:], in_=bk.partition_broadcast(P))
+        for u in range(3, W_BUFS):
+            load(u)
+        for g in range(2):
+            nc.vector.tensor_copy(out=tok_grp[:, g].rearrange("p (c i) t -> p c t i", i=4),
+                                  in_=tok_raw[:, g].rearrange("p t (c i) -> p c t i", i=4))
+        nc.vector.quantize_mx(out=tok_codes[:].rearrange("p g c -> p (g c)").bitcast(FP8X4),
+                              scales=tok_scl[:].rearrange("p g c -> p (g c)"),
+                              in_=tok_grp[:].rearrange("p g c t -> p (g c t)"))
+        for u in range(AHEAD):
+            transposes(u)
+        for u in range(AHEAD):
+            quant_w(u)
+
+        blocks = [(i, j) for i in range(NCH - 1) for j in range(NCH)]
+        first_step = NCH * H + H
+        for s in range(UNITS):
+            n = s - first_step
+            if s + AHEAD < UNITS:
+                transposes(s + AHEAD)
+            products(s)
+            if n >= 0:
+                scores(*blocks[n])
+            add_bias(s)
+            if n >= 0:
+                shift(*blocks[n])
+            if s + AHEAD < UNITS:
+                quant_w(s + AHEAD)
+            quant_qk(s)
+            if s + W_BUFS < UNITS:
+                load(s + W_BUFS)
+            if s == 4:
+                nc.sync.dma_start(out=bias["q"][:], in_=bq.partition_broadcast(P))
+            if n >= 1:
+                expo(*blocks[n - 1])
+                total(*blocks[n - 1])
+            if n >= 2 and (n - 2) % NCH == NCH - 1:
+                invert((n - 2) // NCH)
+            if n >= 6:
+                scale_block(blocks[n - 6][0], blocks[n - 6][1], nc.gpsimd)
+        last = NCH - 1
+        expo(last - 1, NCH - 1)
+        total(last - 1, NCH - 1)
+        scores(last, 0)
+        for j in range(NCH):
+            if j + 1 < NCH:
+                scores(last, j + 1)
+            shift(last, j)
+            expo(last, j)
+            total(last, j)
+            if j == 1:
+                scale_block(last - 2, 2, nc.vector)
+            if j == 2:
+                scale_block(last - 2, 3, nc.vector)
+        lns = {}
+        for i in (last - 1, last):
+            lns[i] = soft.tile([P, NCH, P], F32, name="lns")
+            nc.scalar.activation(out=lns[i][:], in_=sums[i][:], func=ACT.Ln)
+        for i in (last - 1, last):
+            nc.scalar.activation(out=rinv[i][:], in_=lns[i][:], func=ACT.Exp, scale=-1.0)
+        for i in (last - 1, last):
+            for j in range(NCH):
+                scale_block(i, j, nc.gpsimd if j == 0 else nc.vector)

@@ -19,6 +19,11 @@ D = 1024
 NCH = 4
 UNITS = 2 * NCH * H
 W_BUFS = 8
+PE_FROM = 2
+OFFLOAD = ()
+OFF_UNTIL = 14
+QK_BUFS = 2
+MAXB = 5
 AHEAD = 2
 
 FLOPS = 2 * (2 * H * D) * D * L + 2 * H * L * L * D
@@ -38,10 +43,11 @@ def tile_selfattention_pa_kernel(tc, tokens, Wq, bq, Wk, bk, out):
 
         w_src = {"k": Wk.rearrange("(i l h e) k -> i h l (e k)", i=NCH, l=P, h=H, e=2),
                  "q": Wq.rearrange("(i l h e) k -> i h l (e k)", i=NCH, l=P, h=H, e=2)}
+        b_src = {"k": bk, "q": bq}
         out_v = out.rearrange("h (i p) (j m) -> i j p h m", p=P, m=P)
 
         def unit(u):
-            return ("k" if u < NCH * H else "q"), (u // H) % NCH, u % H
+            return ("k" if (u // H) % 2 == 0 else "q"), u // (2 * H), u % H
 
         ident = const.tile([P, P], F32, name="ident")
         make_identity(nc, ident[:])
@@ -67,24 +73,37 @@ def tile_selfattention_pa_kernel(tc, tokens, Wq, bq, Wk, bk, out):
             w_raw[u] = wraw_pool.tile([P, 2, D], BF16, name="w_raw")
             nc.sync.dma_start(out=w_raw[u][:].rearrange("p e k -> p (e k)"), in_=w_src[which][i, h])
 
+        def load_bias(which, i):
+            nc.sync.dma_start(out=bias[which][:, 2 * H * P * i:2 * H * P * (i + 1)],
+                              in_=b_src[which][2 * H * P * i:2 * H * P * (i + 1)].partition_broadcast(P))
+
         def transposes(u):
             w32 = w_raw[u][:].bitcast(F32)
-            wt_grp[u] = stage.tile([P, 2, 4 * 2 * P], BF16, name="wt_grp", align_bytes=64)
+            if u % 2 == 0:
+                wt_grp[u // 2] = stage.tile([P, 2, 2, 4 * 2 * P], BF16, name="wt_grp", bufs=2, align_bytes=64)
             for g in range(2):
                 bank = ps_t.tile([P, 4 * P], F32, name="bank_t")
                 for e in range(2):
                     for v in range(2):
                         nc.tensor.transpose(out=bank[:, (2 * e + v) * P:(2 * e + v + 1) * P],
                                             in_=w32[:, e, 256 * g + P * v:256 * g + P * (v + 1)], identity=ident[:])
-                nc.scalar.copy(out=wt_grp[u][:, g, :].bitcast(F32).rearrange("p (e l v) -> p e l v", e=2, v=2),
+                nc.scalar.copy(out=wt_grp[u // 2][:, u % 2, g, :].bitcast(F32).rearrange("p (e l v) -> p e l v", e=2, v=2),
                                in_=bank[:].rearrange("p (e v l) -> p e l v", e=2, v=2))
 
-        def quant_w(u):
-            w_codes[u] = stage.tile([P, 2, 2 * P], U32, name="w_codes", align_bytes=64)
-            w_scl[u] = stage.tile([P, 2, 2 * P], U8, name="w_scl", align_bytes=64)
-            nc.vector.quantize_mx(out=w_codes[u][:].rearrange("p g c -> p (g c)").bitcast(FP8X4),
-                                  scales=w_scl[u][:].rearrange("p g c -> p (g c)"),
-                                  in_=wt_grp[u][:].rearrange("p g x -> p (g x)"))
+        def quant_w(t):
+            w_codes[t] = stage.tile([P, 2, 2, 2 * P], U32, name="w_codes", align_bytes=64)
+            w_scl[t] = stage.tile([P, 2, 2, 2 * P], U8, name="w_scl", align_bytes=64)
+            nc.vector.quantize_mx(out=w_codes[t][:].rearrange("p x g c -> p (x g c)").bitcast(FP8X4),
+                                  scales=w_scl[t][:].rearrange("p x g c -> p (x g c)"),
+                                  in_=wt_grp[t][:].rearrange("p x g c -> p (x g c)"))
+
+        def quant_w_half(t, x):
+            if x == 0:
+                w_codes[t] = stage.tile([P, 2, 2, 2 * P], U32, name="w_codes", align_bytes=64)
+                w_scl[t] = stage.tile([P, 2, 2, 2 * P], U8, name="w_scl", align_bytes=64)
+            nc.vector.quantize_mx(out=w_codes[t][:, x].rearrange("p g c -> p (g c)").bitcast(FP8X4),
+                                  scales=w_scl[t][:, x].rearrange("p g c -> p (g c)"),
+                                  in_=wt_grp[t][:, x].rearrange("p g c -> p (g c)"))
 
         def products(u):
             banks_m[u] = []
@@ -97,31 +116,42 @@ def tile_selfattention_pa_kernel(tc, tokens, Wq, bq, Wk, bk, out):
                         nc.tensor.matmul_mx(out=bank[:, 2 * P * b:2 * P * (b + 1)],
                                             lhsT=tok_codes[:, g, P * cb:P * (cb + 1)].bitcast(FP8X4),
                                             lhsT_scale=tok_scl[:, g, P * cb:P * (cb + 1)],
-                                            rhs=w_codes[u][:, g, :].bitcast(FP8X4), rhs_scale=w_scl[u][:, g, :],
+                                            rhs=w_codes[u // 2][:, u % 2, g, :].bitcast(FP8X4),
+                                            rhs_scale=w_scl[u // 2][:, u % 2, g, :],
                                             start=(g == 0), stop=(g == 1))
 
         def add_bias(u):
             which, i, h = unit(u)
-            qk_grp[u] = stage.tile([P, 2, P, 2, 2], BF16, name="qk_grp", align_bytes=64)
+            if u % 2 == 0:
+                qk_grp[u // 2] = stage.tile([P, 2, 2, P, 2, 2], BF16, name="qk_grp", bufs=QK_BUFS, align_bytes=64)
             b_v = bias[which][:].rearrange("p (i l h e) -> p i h l e", i=NCH, l=P, h=H, e=2)[:, i, h]
             for a in range(2):
-                nc.vector.tensor_tensor(out=qk_grp[u][:, a],
-                                        in0=banks_m[u][a][:].rearrange("p (b e l) -> p l b e", b=2, e=2),
-                                        in1=b_v.unsqueeze(2).to_broadcast([P, P, 2, 2]), op=ALU.add)
+                if (u % 2, a) in OFFLOAD and u // 2 < OFF_UNTIL:
+                    plain = stage.tile([P, P, 2, 2], F32, name="plain", bufs=2)
+                    nc.scalar.copy(out=plain[:], in_=banks_m[u][a][:].rearrange("p (b e l) -> p l b e", b=2, e=2))
+                    nc.gpsimd.tensor_tensor(out=qk_grp[u // 2][:, u % 2, a], in0=plain[:],
+                                            in1=b_v.unsqueeze(2).to_broadcast([P, P, 2, 2]), op=ALU.add)
+                else:
+                    nc.vector.tensor_tensor(out=qk_grp[u // 2][:, u % 2, a],
+                                            in0=banks_m[u][a][:].rearrange("p (b e l) -> p l b e", b=2, e=2),
+                                            in1=b_v.unsqueeze(2).to_broadcast([P, P, 2, 2]), op=ALU.add)
 
-        def quant_qk(u):
-            which, i, h = unit(u)
-            nc.vector.quantize_mx(out=codes[which][:, i, h].rearrange("p a l -> p (a l)").bitcast(FP8X4),
-                                  scales=scl[which][:, i, h].rearrange("p a l -> p (a l)"),
-                                  in_=qk_grp[u][:].rearrange("p a l b e -> p (a l b e)"))
+        def quant_qk(t):
+            which, i, h = unit(2 * t)
+            nc.vector.quantize_mx(out=codes[which][:, i, h:h + 2].rearrange("p x a l -> p (x a l)").bitcast(FP8X4),
+                                  scales=scl[which][:, i, h:h + 2].rearrange("p x a l -> p (x a l)"),
+                                  in_=qk_grp[t][:].rearrange("p x a l b e -> p (x a l b e)"))
 
         bank_s = {}
         e_t = {}
         sums = {}
         rinv = {}
 
-        def scores(i, j):
-            bank_s[i, j] = ps_s.tile([P, H, P], F32, name="bank_s")
+        def scores(i, j, pool=None):
+            if pool is None:
+                bank_s[i, j] = ps_s.tile([P, H, P], F32, name="bank_s")
+            else:
+                bank_s[i, j] = pool.tile([P, H, P], F32, name="bank_t")
             for h in range(H):
                 for a in range(2):
                     nc.tensor.matmul_mx(out=bank_s[i, j][:, h, :],
@@ -132,96 +162,145 @@ def tile_selfattention_pa_kernel(tc, tokens, Wq, bq, Wk, bk, out):
         def shift(i, j):
             mx = soft.tile([P, P], F32, name="mx")
             nc.vector.tensor_reduce(out=mx[:], in_=bank_s[i, j][:].rearrange("p h m -> p m h"), axis=AX.X, op=ALU.max)
-            e_t[i, j] = soft.tile([P, H, P], F32, name="e_t", bufs=12)
+            e_t[i, j] = soft.tile([P, H, P], F32, name="e_t", bufs=10)
             nc.vector.tensor_tensor(out=e_t[i, j][:], in0=bank_s[i, j][:],
                                     in1=mx[:].unsqueeze(1).to_broadcast([P, H, P]), op=ALU.subtract)
 
         def expo(i, j):
             nc.scalar.activation(out=e_t[i, j][:], in_=e_t[i, j][:], func=ACT.Exp, scale=1.0 / 32.0)
 
+        sum_ps = {}
+        place = {}
+
         def total(i, j):
-            if j == 0:
-                sums[i] = soft.tile([P, NCH, P], F32, name="sums", bufs=3)
-                rinv[i] = soft.tile([P, NCH, P], F32, name="rinv", bufs=3)
+            n, c = place[i, j]
+            if c == 0:
+                sums[n] = soft.tile([P, MAXB, P], F32, name="sums")
+                rinv[n] = soft.tile([P, MAXB, P], F32, name="rinv")
             half = soft.tile([P, 2, P], F32, name="half")
             nc.gpsimd.tensor_tensor(out=half[:], in0=e_t[i, j][:, 0:2, :], in1=e_t[i, j][:, 2:4, :], op=ALU.add)
-            nc.gpsimd.tensor_tensor(out=sums[i][:, j, :], in0=half[:, 0, :], in1=half[:, 1, :], op=ALU.add)
+            nc.gpsimd.tensor_tensor(out=sums[n][:, c, :], in0=half[:, 0, :], in1=half[:, 1, :], op=ALU.add)
 
-        def invert(i):
-            lns = soft.tile([P, NCH, P], F32, name="lns")
-            nc.scalar.activation(out=lns[:], in_=sums[i][:], func=ACT.Ln)
-            nc.scalar.activation(out=rinv[i][:], in_=lns[:], func=ACT.Exp, scale=-1.0)
+        def total_pe(i, j, own_bank):
+            n, c = place[i, j]
+            if c == 0:
+                rinv[n] = soft.tile([P, MAXB, P], F32, name="rinv")
+            if own_bank:
+                sum_ps[i, j] = ps_m.tile([P, 4 * P], F32, name="bank_m")[:, 0:P]
+            else:
+                if c == 0:
+                    sums[n] = ps_t.tile([P, 4, P], F32, name="bank_t")
+                sum_ps[i, j] = sums[n][:, c, :]
+            for h in range(H):
+                nc.tensor.matmul(out=sum_ps[i, j], lhsT=ident[:], rhs=e_t[i, j][:, h, :], start=(h == 0), stop=(h == H - 1))
+
+        def invert(n, size):
+            lns = soft.tile([P, MAXB, P], F32, name="lns")
+            nc.scalar.activation(out=lns[:, 0:size, :], in_=sums[n][:, 0:size, :], func=ACT.Ln)
+            nc.scalar.activation(out=rinv[n][:, 0:size, :], in_=lns[:, 0:size, :], func=ACT.Exp, scale=-1.0)
+
+        def invert_block(i, j):
+            n, c = place[i, j]
+            nc.vector.reciprocal(out=rinv[n][:, c, :], in_=sum_ps[i, j])
 
         def scale_block(i, j, eng):
+            n, c = place[i, j]
             eng.tensor_tensor(out=e_t[i, j][:], in0=e_t[i, j][:],
-                              in1=rinv[i][:, j, :].unsqueeze(1).to_broadcast([P, H, P]), op=ALU.mult)
+                              in1=rinv[n][:, c, :].unsqueeze(1).to_broadcast([P, H, P]), op=ALU.mult)
             nc.sync.dma_start(out=out_v[i, j], in_=e_t[i, j][:])
 
         tok_src = tokens.rearrange("(g v p e) c -> g p v (e c)", g=2, v=2, p=P, e=2)
         for g in range(2):
             nc.sync.dma_start(out=tok_raw[:, g].rearrange("p (v e) c -> p v (e c)", v=2), in_=tok_src[g])
-        for u in range(3):
+        load(0)
+        load(1)
+        load_bias("k", 0)
+        for u in range(2, W_BUFS):
             load(u)
-        nc.sync.dma_start(out=bias["k"][:], in_=bk.partition_broadcast(P))
-        for u in range(3, W_BUFS):
-            load(u)
+            if u == 3:
+                load_bias("q", 0)
         for g in range(2):
             nc.vector.tensor_copy(out=tok_grp[:, g].rearrange("p (c i) t -> p c t i", i=4),
                                   in_=tok_raw[:, g].rearrange("p t (c i) -> p c t i", i=4))
         nc.vector.quantize_mx(out=tok_codes[:].rearrange("p g c -> p (g c)").bitcast(FP8X4),
                               scales=tok_scl[:].rearrange("p g c -> p (g c)"),
                               in_=tok_grp[:].rearrange("p g c t -> p (g c t)"))
-        for u in range(AHEAD):
-            transposes(u)
-        for u in range(AHEAD):
-            quant_w(u)
 
-        blocks = [(i, j) for i in range(NCH - 1) for j in range(NCH)]
-        first_step = NCH * H + H
-        for s in range(UNITS):
-            n = s - first_step
-            if s + AHEAD < UNITS:
-                transposes(s + AHEAD)
-            products(s)
-            if n >= 0:
-                scores(*blocks[n])
-            add_bias(s)
-            if n >= 0:
-                shift(*blocks[n])
-            if s + AHEAD < UNITS:
-                quant_w(s + AHEAD)
-            quant_qk(s)
-            if s + W_BUFS < UNITS:
-                load(s + W_BUFS)
-            if s == 4:
-                nc.sync.dma_start(out=bias["q"][:], in_=bq.partition_broadcast(P))
-            if n >= 1:
-                expo(*blocks[n - 1])
-                total(*blocks[n - 1])
-            if n >= 2 and (n - 2) % NCH == NCH - 1:
-                invert((n - 2) // NCH)
-            if n >= 6:
-                scale_block(blocks[n - 6][0], blocks[n - 6][1], nc.gpsimd)
-        last = NCH - 1
-        expo(last - 1, NCH - 1)
-        total(last - 1, NCH - 1)
-        scores(last, 0)
-        for j in range(NCH):
-            if j + 1 < NCH:
-                scores(last, j + 1)
-            shift(last, j)
-            expo(last, j)
-            total(last, j)
-            if j == 1:
-                scale_block(last - 2, 2, nc.vector)
-            if j == 2:
-                scale_block(last - 2, 3, nc.vector)
-        lns = {}
-        for i in (last - 1, last):
-            lns[i] = soft.tile([P, NCH, P], F32, name="lns")
-            nc.scalar.activation(out=lns[i][:], in_=sums[i][:], func=ACT.Ln)
-        for i in (last - 1, last):
-            nc.scalar.activation(out=rinv[i][:], in_=lns[i][:], func=ACT.Exp, scale=-1.0)
-        for i in (last - 1, last):
-            for j in range(NCH):
-                scale_block(i, j, nc.gpsimd if j == 0 else nc.vector)
+        def fetch_after(u):
+            if u + W_BUFS < UNITS:
+                load(u + W_BUFS)
+            if u % H == 0 and u >= 2 * H:
+                load_bias(unit(u)[0], unit(u)[1])
+
+        def ahead(u):
+            if u < UNITS:
+                transposes(u)
+                fetch_after(u)
+
+        work = {}
+        for c in range(1, 2 * NCH):
+            if c % 2 == 1:
+                work[2 * c + 2] = [(c // 2, j) for j in range(c // 2 + 1)]
+            else:
+                work[2 * c + 2] = [(i, c // 2) for i in range(c // 2)]
+        batches = [[4, 6, 8], [10, 12], [14], [16]]
+        inv_at = {}
+        for n in range(len(batches)):
+            members = [b for t in batches[n] for b in work[t]]
+            for c in range(len(members)):
+                place[members[c]] = (n, c)
+            inv_at[batches[n][-1] + 1] = (n, members)
+
+        pairs = UNITS // 2
+        late = []
+        ahead(0)
+        quant_w_half(0, 0)
+        ahead(1)
+        quant_w_half(0, 1)
+        for t in range(pairs):
+            todo = work.get(t, [])
+            for x in range(2):
+                u = 2 * t + x
+                if t == 0:
+                    ahead(2 + x)
+                else:
+                    ahead(u + 2 * AHEAD)
+                products(u)
+                if x == 1:
+                    for b in late:
+                        total_pe(b[0], b[1], False)
+                    late = []
+                mine = todo[0:2] if x == 0 else todo[2:]
+                for b in mine:
+                    scores(b[0], b[1])
+                add_bias(u)
+                for b in mine:
+                    shift(b[0], b[1])
+            if t in inv_at:
+                invert(inv_at[t][0], len(inv_at[t][1]))
+            for b in todo:
+                expo(b[0], b[1])
+                if place[b][0] >= PE_FROM:
+                    late.append(b)
+                else:
+                    total(b[0], b[1])
+            if t == 0:
+                ahead(4)
+                ahead(5)
+                quant_w(1)
+            if t + AHEAD < pairs:
+                quant_w(t + AHEAD)
+            quant_qk(t)
+            if t in inv_at:
+                for b in inv_at[t][1]:
+                    scale_block(b[0], b[1], nc.gpsimd)
+        last = work[pairs]
+        for c in range(len(last)):
+            scores(last[c][0], last[c][1], None if c < 2 else ps_t)
+        for c in range(len(last)):
+            shift(last[c][0], last[c][1])
+            expo(last[c][0], last[c][1])
+            total_pe(last[c][0], last[c][1], True)
+        for c in range(len(last)):
+            invert_block(last[c][0], last[c][1])
+            scale_block(last[c][0], last[c][1], nc.vector if c == len(last) - 1 else nc.gpsimd)

@@ -7,6 +7,7 @@ F32 = mybir.dt.float32
 BF16 = mybir.dt.bfloat16
 U32 = mybir.dt.uint32
 U8 = mybir.dt.uint8
+I32 = mybir.dt.int32
 FP8X4 = mybir.dt.float8_e4m3fn_x4
 ALU = mybir.AluOpType
 ACT = mybir.ActivationFunctionType
@@ -43,14 +44,11 @@ def tile_selfattention_pa_kernel(tc, tokens, Wq, bq, Wk, bk, out):
 
         w_src = {"k": Wk.rearrange("(i l h e) k -> i h l (e k)", i=NCH, l=P, h=H, e=2),
                  "q": Wq.rearrange("(i l h e) k -> i h l (e k)", i=NCH, l=P, h=H, e=2)}
-        b_src = {"k": bk, "q": bq}
         out_v = out.rearrange("h (i p) (j m) -> i j p h m", p=P, m=P)
 
         def unit(u):
             return ("k" if (u // H) % 2 == 0 else "q"), u // (2 * H), u % H
 
-        ident = const.tile([P, P], F32, name="ident")
-        make_identity(nc, ident[:])
         tok_raw = const.tile([P, 2, 4, L], BF16, name="tok_raw")
         tok_grp = const.tile([P, 2, L, 4], BF16, name="tok_grp", align_bytes=64)
         tok_codes = const.tile([P, 2, L], U32, name="tok_codes", align_bytes=64)
@@ -60,6 +58,16 @@ def tile_selfattention_pa_kernel(tc, tokens, Wq, bq, Wk, bk, out):
                  "q": const.tile([P, NCH, H, 2, P], U32, name="q_codes", align_bytes=64)}
         scl = {"k": const.tile([P, NCH, H, 2, P], U8, name="k_scl", align_bytes=64),
                "q": const.tile([P, NCH, H, 2, P], U8, name="q_scl", align_bytes=64)}
+
+        b_rows = const.tile([P, 2 * P], BF16, name="b_rows")
+        nc.vector.memset(b_rows[32:64, :].bitcast(I32), 0)
+        nc.vector.memset(b_rows[64:128, :].bitcast(I32), 0)
+        nc.scalar.dma_start(out=b_rows[0:16, :], in_=bk.rearrange("(r n) -> r n", n=2 * P))
+        nc.scalar.dma_start(out=b_rows[16:32, :], in_=bq.rearrange("(r n) -> r n", n=2 * P))
+        ident = const.tile([P, P], F32, name="ident")
+        make_identity(nc, ident[:])
+        ident_b = const.tile([P, P], BF16, name="ident_b")
+        make_identity(nc, ident_b[:])
 
         w_raw = {}
         wt_grp = {}
@@ -73,9 +81,19 @@ def tile_selfattention_pa_kernel(tc, tokens, Wq, bq, Wk, bk, out):
             w_raw[u] = wraw_pool.tile([P, 2, D], BF16, name="w_raw")
             nc.sync.dma_start(out=w_raw[u][:].rearrange("p e k -> p (e k)"), in_=w_src[which][i, h])
 
-        def load_bias(which, i):
-            nc.sync.dma_start(out=bias[which][:, 2 * H * P * i:2 * H * P * (i + 1)],
-                              in_=b_src[which][2 * H * P * i:2 * H * P * (i + 1)].partition_broadcast(P))
+        def fetch_bias(which, i):
+            src = bk if which == "k" else bq
+            nc.scalar.dma_start(out=bias[which][:, 2 * H * P * i:2 * H * P * (i + 1)],
+                                in_=src[2 * H * P * i:2 * H * P * (i + 1)].partition_broadcast(P))
+
+        def spread_bias(which, i, pool, name):
+            for half in range(2):
+                bank = pool.tile([P, 4 * P], F32, name=name)
+                for z in range(2):
+                    r = (0 if which == "k" else 16) + 4 * i + 2 * half + z
+                    nc.tensor.matmul(out=bank[:, 2 * P * z:2 * P * (z + 1)], lhsT=ident_b[:, r:r + 1].to_broadcast([P, P]),
+                                     rhs=b_rows[:], start=True, stop=True)
+                nc.scalar.copy(out=bias[which][:, 4 * P * (2 * i + half):4 * P * (2 * i + half + 1)], in_=bank[:])
 
         def transposes(u):
             w32 = w_raw[u][:].bitcast(F32)
@@ -212,13 +230,8 @@ def tile_selfattention_pa_kernel(tc, tokens, Wq, bq, Wk, bk, out):
         tok_src = tokens.rearrange("(g v p e) c -> g p v (e c)", g=2, v=2, p=P, e=2)
         for g in range(2):
             nc.sync.dma_start(out=tok_raw[:, g].rearrange("p (v e) c -> p v (e c)", v=2), in_=tok_src[g])
-        load(0)
-        load(1)
-        load_bias("k", 0)
-        for u in range(2, W_BUFS):
+        for u in range(W_BUFS):
             load(u)
-            if u == 3:
-                load_bias("q", 0)
         for g in range(2):
             nc.vector.tensor_copy(out=tok_grp[:, g].rearrange("p (c i) t -> p c t i", i=4),
                                   in_=tok_raw[:, g].rearrange("p t (c i) -> p c t i", i=4))
@@ -229,8 +242,7 @@ def tile_selfattention_pa_kernel(tc, tokens, Wq, bq, Wk, bk, out):
         def fetch_after(u):
             if u + W_BUFS < UNITS:
                 load(u + W_BUFS)
-            if u % H == 0 and u >= 2 * H:
-                load_bias(unit(u)[0], unit(u)[1])
+
 
         def ahead(u):
             if u < UNITS:
@@ -257,6 +269,7 @@ def tile_selfattention_pa_kernel(tc, tokens, Wq, bq, Wk, bk, out):
         quant_w_half(0, 0)
         ahead(1)
         quant_w_half(0, 1)
+        spread_bias("k", 0, ps_m, "bank_m")
         for t in range(pairs):
             todo = work.get(t, [])
             for x in range(2):
@@ -276,6 +289,10 @@ def tile_selfattention_pa_kernel(tc, tokens, Wq, bq, Wk, bk, out):
                 add_bias(u)
                 for b in mine:
                     shift(b[0], b[1])
+            if t == 1:
+                spread_bias("q", 0, ps_t, "bank_t")
+            if t % 2 == 0 and t // 2 + 2 < 2 * NCH:
+                fetch_bias(unit(2 * t + 2 * H)[0], unit(2 * t + 2 * H)[1])
             if t in inv_at:
                 invert(inv_at[t][0], len(inv_at[t][1]))
             for b in todo:

@@ -19,13 +19,13 @@ L = 512
 D = 1024
 NCH = 4
 UNITS = 2 * NCH * H
-W_BUFS = 8
-PE_FROM = 2
-OFFLOAD = ()
-OFF_UNTIL = 14
-QK_BUFS = 2
-MAXB = 5
-AHEAD = 2
+W_BUFS = 10
+AHEAD = 4
+ROWS = ()
+TURN_LAG = 2
+EXP_LAG = 1
+BATCHES = ((9, 22, 24), (23, 29, 31), (30, 31, 32))
+MAXB = 6
 
 FLOPS = 2 * (2 * H * D) * D * L + 2 * H * L * L * D
 
@@ -37,13 +37,14 @@ def tile_selfattention_pa_kernel(tc, tokens, Wq, bq, Wk, bk, out):
         wraw_pool = ctx.enter_context(tc.tile_pool(name="wraw", bufs=W_BUFS))
         stage = ctx.enter_context(tc.tile_pool(name="stage", bufs=3))
         soft = ctx.enter_context(tc.tile_pool(name="soft", bufs=2))
-        ps_t = ctx.enter_context(tc.psum_pool(name="ps_t", bufs=2))
-        ps_m = ctx.enter_context(tc.psum_pool(name="ps_m", bufs=4))
-        ps_s = ctx.enter_context(tc.psum_pool(name="ps_s", bufs=2))
+        ps_t = ctx.enter_context(tc.psum_pool(name="ps_t", bufs=4))
+        ps_m = ctx.enter_context(tc.psum_pool(name="ps_m", bufs=3))
+        ps_s = ctx.enter_context(tc.psum_pool(name="ps_s", bufs=1))
         ctx.enter_context(tc.manual_schedule())
 
         w_src = {"k": Wk.rearrange("(i l h e) k -> i h l (e k)", i=NCH, l=P, h=H, e=2),
                  "q": Wq.rearrange("(i l h e) k -> i h l (e k)", i=NCH, l=P, h=H, e=2)}
+        out_row = out[:, L - P:L, :]
         out_v = out.rearrange("h (i p) (j m) -> i j p h m", p=P, m=P)
 
         def unit(u):
@@ -54,6 +55,8 @@ def tile_selfattention_pa_kernel(tc, tokens, Wq, bq, Wk, bk, out):
         tok_codes = const.tile([P, 2, L], U32, name="tok_codes", align_bytes=64)
         tok_scl = const.tile([P, 2, L], U8, name="tok_scl", align_bytes=64)
         bias = {"k": const.tile([P, H * D], BF16, name="bias_k"), "q": const.tile([P, H * D], BF16, name="bias_q")}
+        bias_col = {"k": const.tile([P, NCH, 2 * H], BF16, name="bias_col_k"),
+                    "q": const.tile([P, NCH, 2 * H], BF16, name="bias_col_q")}
         codes = {"k": const.tile([P, NCH, H, 2, P], U32, name="k_codes", align_bytes=64),
                  "q": const.tile([P, NCH, H, 2, P], U32, name="q_codes", align_bytes=64)}
         scl = {"k": const.tile([P, NCH, H, 2, P], U8, name="k_scl", align_bytes=64),
@@ -75,6 +78,7 @@ def tile_selfattention_pa_kernel(tc, tokens, Wq, bq, Wk, bk, out):
         w_scl = {}
         qk_grp = {}
         banks_m = {}
+        rows = {}
 
         def load(u):
             which, i, h = unit(u)
@@ -98,7 +102,7 @@ def tile_selfattention_pa_kernel(tc, tokens, Wq, bq, Wk, bk, out):
         def transposes(u):
             w32 = w_raw[u][:].bitcast(F32)
             if u % 2 == 0:
-                wt_grp[u // 2] = stage.tile([P, 2, 2, 4 * 2 * P], BF16, name="wt_grp", bufs=2, align_bytes=64)
+                wt_grp[u // 2] = stage.tile([P, 2, 2, 4 * 2 * P], BF16, name="wt_grp", align_bytes=64)
             for g in range(2):
                 bank = ps_t.tile([P, 4 * P], F32, name="bank_t")
                 for e in range(2):
@@ -138,32 +142,54 @@ def tile_selfattention_pa_kernel(tc, tokens, Wq, bq, Wk, bk, out):
                                             rhs_scale=w_scl[u // 2][:, u % 2, g, :],
                                             start=(g == 0), stop=(g == 1))
 
+        def products_rows(u):
+            banks_m[u] = []
+            for e in range(2):
+                bank = ps_m.tile([P, 4 * P], F32, name="bank_m")
+                banks_m[u].append(bank)
+                for g in range(2):
+                    nc.tensor.matmul_mx(out=bank[:],
+                                        lhsT=w_codes[u // 2][:, u % 2, g, P * e:P * (e + 1)].bitcast(FP8X4),
+                                        lhsT_scale=w_scl[u // 2][:, u % 2, g, P * e:P * (e + 1)],
+                                        rhs=tok_codes[:, g, :].bitcast(FP8X4), rhs_scale=tok_scl[:, g, :],
+                                        start=(g == 0), stop=(g == 1))
+
+        def add_bias_rows(u):
+            which, i, h = unit(u)
+            rows[u] = stage.tile([P, 2, 2, P, 2], BF16, name="rows", align_bytes=64)
+            for e in range(2):
+                nc.scalar.activation(out=rows[u][:, e], in_=banks_m[u][e][:].rearrange("l (v b p) -> l v p b", v=2, b=2),
+                                     func=ACT.Identity, bias=bias_col[which][:, i, 2 * h + e:2 * h + e + 1])
+
+        def turn(u):
+            words = rows[u][:].rearrange("l e v p b -> l e v (p b)").bitcast(F32)
+            bank = ps_t.tile([P, 4 * P], F32, name="bank_t")
+            for v in range(2):
+                for e in range(2):
+                    nc.tensor.transpose(out=bank[:, (2 * v + e) * P:(2 * v + e + 1) * P], in_=words[:, e, v, :],
+                                        identity=ident[:])
+            nc.scalar.copy(out=qk_grp[u // 2][:, u % 2].rearrange("p a l e b -> p a l (e b)").bitcast(F32),
+                           in_=bank[:].rearrange("p (v e l) -> p v l e", v=2, e=2))
+
         def add_bias(u):
             which, i, h = unit(u)
-            if u % 2 == 0:
-                qk_grp[u // 2] = stage.tile([P, 2, 2, P, 2, 2], BF16, name="qk_grp", bufs=QK_BUFS, align_bytes=64)
             b_v = bias[which][:].rearrange("p (i l h e) -> p i h l e", i=NCH, l=P, h=H, e=2)[:, i, h]
             for a in range(2):
-                if (u % 2, a) in OFFLOAD and u // 2 < OFF_UNTIL:
-                    plain = stage.tile([P, P, 2, 2], F32, name="plain", bufs=2)
-                    nc.scalar.copy(out=plain[:], in_=banks_m[u][a][:].rearrange("p (b e l) -> p l b e", b=2, e=2))
-                    nc.gpsimd.tensor_tensor(out=qk_grp[u // 2][:, u % 2, a], in0=plain[:],
-                                            in1=b_v.unsqueeze(2).to_broadcast([P, P, 2, 2]), op=ALU.add)
-                else:
-                    nc.vector.tensor_tensor(out=qk_grp[u // 2][:, u % 2, a],
-                                            in0=banks_m[u][a][:].rearrange("p (b e l) -> p l b e", b=2, e=2),
-                                            in1=b_v.unsqueeze(2).to_broadcast([P, P, 2, 2]), op=ALU.add)
+                nc.vector.tensor_tensor(out=qk_grp[u // 2][:, u % 2, a],
+                                        in0=banks_m[u][a][:].rearrange("p (b e l) -> p l e b", b=2, e=2),
+                                        in1=b_v.unsqueeze(3).to_broadcast([P, P, 2, 2]), op=ALU.add)
 
         def quant_qk(t):
             which, i, h = unit(2 * t)
             nc.vector.quantize_mx(out=codes[which][:, i, h:h + 2].rearrange("p x a l -> p (x a l)").bitcast(FP8X4),
                                   scales=scl[which][:, i, h:h + 2].rearrange("p x a l -> p (x a l)"),
-                                  in_=qk_grp[t][:].rearrange("p x a l b e -> p (x a l b e)"))
+                                  in_=qk_grp[t][:].rearrange("p x a l e b -> p (x a l e b)"))
 
         bank_s = {}
         e_t = {}
         sums = {}
         rinv = {}
+        place = {}
 
         def scores(i, j, pool=None):
             if pool is None:
@@ -180,46 +206,26 @@ def tile_selfattention_pa_kernel(tc, tokens, Wq, bq, Wk, bk, out):
         def shift(i, j):
             mx = soft.tile([P, P], F32, name="mx")
             nc.vector.tensor_reduce(out=mx[:], in_=bank_s[i, j][:].rearrange("p h m -> p m h"), axis=AX.X, op=ALU.max)
-            e_t[i, j] = soft.tile([P, H, P], F32, name="e_t", bufs=10)
+            e_t[i, j] = soft.tile([P, H, P], F32, name="e_t", bufs=12)
             nc.vector.tensor_tensor(out=e_t[i, j][:], in0=bank_s[i, j][:],
                                     in1=mx[:].unsqueeze(1).to_broadcast([P, H, P]), op=ALU.subtract)
 
         def expo(i, j):
             nc.scalar.activation(out=e_t[i, j][:], in_=e_t[i, j][:], func=ACT.Exp, scale=1.0 / 32.0)
 
-        sum_ps = {}
-        place = {}
-
         def total(i, j):
             n, c = place[i, j]
             if c == 0:
                 sums[n] = soft.tile([P, MAXB, P], F32, name="sums")
-                rinv[n] = soft.tile([P, MAXB, P], F32, name="rinv")
             half = soft.tile([P, 2, P], F32, name="half")
             nc.gpsimd.tensor_tensor(out=half[:], in0=e_t[i, j][:, 0:2, :], in1=e_t[i, j][:, 2:4, :], op=ALU.add)
-            nc.gpsimd.tensor_tensor(out=sums[n][:, c, :], in0=half[:, 0, :], in1=half[:, 1, :], op=ALU.add)
-
-        def total_pe(i, j, own_bank):
-            n, c = place[i, j]
-            if c == 0:
-                rinv[n] = soft.tile([P, MAXB, P], F32, name="rinv")
-            if own_bank:
-                sum_ps[i, j] = ps_m.tile([P, 4 * P], F32, name="bank_m")[:, 0:P]
-            else:
-                if c == 0:
-                    sums[n] = ps_t.tile([P, 4, P], F32, name="bank_t")
-                sum_ps[i, j] = sums[n][:, c, :]
-            for h in range(H):
-                nc.tensor.matmul(out=sum_ps[i, j], lhsT=ident[:], rhs=e_t[i, j][:, h, :], start=(h == 0), stop=(h == H - 1))
+            whole = soft.tile([P, P], F32, name="whole")
+            nc.gpsimd.tensor_tensor(out=whole[:], in0=half[:, 0, :], in1=half[:, 1, :], op=ALU.add)
+            nc.gpsimd.tensor_tensor(out=sums[n][:, c, :], in0=whole[:], in1=whole[:], op=ALU.mult)
 
         def invert(n, size):
-            lns = soft.tile([P, MAXB, P], F32, name="lns")
-            nc.scalar.activation(out=lns[:, 0:size, :], in_=sums[n][:, 0:size, :], func=ACT.Ln)
-            nc.scalar.activation(out=rinv[n][:, 0:size, :], in_=lns[:, 0:size, :], func=ACT.Exp, scale=-1.0)
-
-        def invert_block(i, j):
-            n, c = place[i, j]
-            nc.vector.reciprocal(out=rinv[n][:, c, :], in_=sum_ps[i, j])
+            rinv[n] = soft.tile([P, MAXB, P], F32, name="rinv")
+            nc.scalar.activation(out=rinv[n][:, 0:size, :], in_=sums[n][:, 0:size, :], func=ACT.Abs_reciprocal_sqrt)
 
         def scale_block(i, j, eng):
             n, c = place[i, j]
@@ -228,96 +234,133 @@ def tile_selfattention_pa_kernel(tc, tokens, Wq, bq, Wk, bk, out):
             nc.sync.dma_start(out=out_v[i, j], in_=e_t[i, j][:])
 
         tok_src = tokens.rearrange("(g v p e) c -> g p v (e c)", g=2, v=2, p=P, e=2)
-        for g in range(2):
+        def load_tokens(g):
             nc.sync.dma_start(out=tok_raw[:, g].rearrange("p (v e) c -> p v (e c)", v=2), in_=tok_src[g])
-        for u in range(W_BUFS):
+
+        def token_half(z):
+            cols = slice(L // 2 * z, L // 2 * (z + 1))
+            for g in range(2):
+                nc.vector.tensor_copy(out=tok_grp[:, g, cols].rearrange("p (c i) t -> p c t i", i=4),
+                                      in_=tok_raw[:, g, :, cols].rearrange("p t (c i) -> p c t i", i=4))
+            for g in range(2):
+                nc.vector.quantize_mx(out=tok_codes[:, g, cols].bitcast(FP8X4), scales=tok_scl[:, g, cols],
+                                      in_=tok_grp[:, g, cols].rearrange("p c t -> p (c t)"))
+
+        for z in range(1):
+            load(z)
+        load_tokens(0)
+        load_tokens(1)
+        for u in range(1, W_BUFS):
             load(u)
-        for g in range(2):
-            nc.vector.tensor_copy(out=tok_grp[:, g].rearrange("p (c i) t -> p c t i", i=4),
-                                  in_=tok_raw[:, g].rearrange("p t (c i) -> p c t i", i=4))
-        nc.vector.quantize_mx(out=tok_codes[:].rearrange("p g c -> p (g c)").bitcast(FP8X4),
-                              scales=tok_scl[:].rearrange("p g c -> p (g c)"),
-                              in_=tok_grp[:].rearrange("p g c t -> p (g c t)"))
-
-        def fetch_after(u):
-            if u + W_BUFS < UNITS:
-                load(u + W_BUFS)
-
+            if u == 2 and len(ROWS) > 0:
+                for which, b in (("k", bk), ("q", bq)):
+                    nc.sync.dma_start(out=bias_col[which][:], in_=b.rearrange("(i l n) -> l i n", i=NCH, l=P))
 
         def ahead(u):
             if u < UNITS:
                 transposes(u)
-                fetch_after(u)
+                if u + W_BUFS < UNITS:
+                    load(u + W_BUFS)
 
         work = {}
-        for c in range(1, 2 * NCH):
-            if c % 2 == 1:
-                work[2 * c + 2] = [(c // 2, j) for j in range(c // 2 + 1)]
-            else:
-                work[2 * c + 2] = [(i, c // 2) for i in range(c // 2)]
-        batches = [[4, 6, 8], [10, 12], [14], [16]]
+        for c in range(1, 2 * NCH - 1):
+            done = [(c // 2, j) for j in range(c // 2 + 1)] if c % 2 == 1 else [(i, c // 2) for i in range(c // 2)]
+            for n in range(len(done)):
+                work[H * (c + 1) + 1 + n] = done[n]
         inv_at = {}
-        for n in range(len(batches)):
-            members = [b for t in batches[n] for b in work[t]]
+        for n in range(len(BATCHES)):
+            first, end, at = BATCHES[n]
+            members = [work[u] for u in range(first, end + 1) if u in work]
             for c in range(len(members)):
                 place[members[c]] = (n, c)
-            inv_at[batches[n][-1] + 1] = (n, members)
+            inv_at[at] = (n, members)
 
-        pairs = UNITS // 2
-        late = []
+        def softmax_end(u):
+            if u - EXP_LAG in work:
+                expo(work[u - EXP_LAG][0], work[u - EXP_LAG][1])
+                total(work[u - EXP_LAG][0], work[u - EXP_LAG][1])
+            if u in inv_at and u < UNITS:
+                n, members = inv_at[u]
+                invert(n, len(members))
+                for b in members:
+                    scale_block(b[0], b[1], nc.gpsimd)
+
+        ready = {}
+        for t in range(UNITS // 2):
+            at = max(u + TURN_LAG if u in ROWS else u for u in (2 * t, 2 * t + 1))
+            ready.setdefault(at, []).append(t)
+
         ahead(0)
+        token_half(0)
         quant_w_half(0, 0)
-        ahead(1)
-        quant_w_half(0, 1)
         spread_bias("k", 0, ps_m, "bank_m")
-        for t in range(pairs):
-            todo = work.get(t, [])
-            for x in range(2):
-                u = 2 * t + x
-                if t == 0:
-                    ahead(2 + x)
-                else:
-                    ahead(u + 2 * AHEAD)
-                products(u)
-                if x == 1:
-                    for b in late:
-                        total_pe(b[0], b[1], False)
-                    late = []
-                mine = todo[0:2] if x == 0 else todo[2:]
-                for b in mine:
-                    scores(b[0], b[1])
-                add_bias(u)
-                for b in mine:
-                    shift(b[0], b[1])
-            if t == 1:
-                spread_bias("q", 0, ps_t, "bank_t")
-            if t % 2 == 0 and t // 2 + 2 < 2 * NCH:
-                fetch_bias(unit(2 * t + 2 * H)[0], unit(2 * t + 2 * H)[1])
-            if t in inv_at:
-                invert(inv_at[t][0], len(inv_at[t][1]))
-            for b in todo:
-                expo(b[0], b[1])
-                if place[b][0] >= PE_FROM:
-                    late.append(b)
-                else:
-                    total(b[0], b[1])
-            if t == 0:
+        ahead(1)
+        token_half(1)
+        quant_w_half(0, 1)
+        for u in range(UNITS):
+            if u == 0:
+                ahead(2)
+            elif u == 1:
+                ahead(3)
                 ahead(4)
                 ahead(5)
+            else:
+                ahead(u + AHEAD)
+            if u - TURN_LAG in ROWS:
+                turn(u - TURN_LAG)
+            if u % 2 == 0:
+                qk_grp[u // 2] = stage.tile([P, 2, 2, P, 2, 2], BF16, name="qk_grp", bufs=4, align_bytes=64)
+            if u in ROWS:
+                products_rows(u)
+            else:
+                products(u)
+            if u in work:
+                scores(work[u][0], work[u][1])
+            if u in ROWS:
+                add_bias_rows(u)
+            else:
+                add_bias(u)
+            if u in work:
+                shift(work[u][0], work[u][1])
+            softmax_end(u)
+            if u == 3:
+                spread_bias("q", 0, ps_t, "bank_t")
+            if u % 4 == 1 and u // 4 + 2 < 2 * NCH:
+                fetch_bias(unit(u // 4 * 4 + 2 * H)[0], unit(u // 4 * 4 + 2 * H)[1])
+            if u == 1:
                 quant_w(1)
-            if t + AHEAD < pairs:
-                quant_w(t + AHEAD)
-            quant_qk(t)
-            if t in inv_at:
-                for b in inv_at[t][1]:
-                    scale_block(b[0], b[1], nc.gpsimd)
-        last = work[pairs]
-        for c in range(len(last)):
-            scores(last[c][0], last[c][1], None if c < 2 else ps_t)
-        for c in range(len(last)):
-            shift(last[c][0], last[c][1])
-            expo(last[c][0], last[c][1])
-            total_pe(last[c][0], last[c][1], True)
-        for c in range(len(last)):
-            invert_block(last[c][0], last[c][1])
-            scale_block(last[c][0], last[c][1], nc.vector if c == len(last) - 1 else nc.gpsimd)
+            if u % 2 == 1 and u + AHEAD < UNITS:
+                quant_w(u // 2 + AHEAD // 2)
+            for t in ready.get(u, []):
+                quant_qk(t)
+        for u in range(UNITS, UNITS + TURN_LAG):
+            if u - TURN_LAG in ROWS:
+                turn(u - TURN_LAG)
+            for t in ready.get(u, []):
+                quant_qk(t)
+        e_last = soft.tile([P, H, NCH, P], F32, name="e_last", bufs=1)
+        rinv_last = soft.tile([P, NCH, P], F32, name="rinv_last", bufs=1)
+        roots_last = soft.tile([P, NCH, P], F32, name="roots_last", bufs=1)
+        for j in range(NCH):
+            scores(NCH - 1, j, ps_t)
+        sum_bank = ps_m.tile([P, NCH, P], F32, name="bank_m")
+        for u in range(UNITS, UNITS + EXP_LAG):
+            softmax_end(u)
+        for j in range(NCH):
+            mx = soft.tile([P, P], F32, name="mx")
+            bank = bank_s[NCH - 1, j]
+            nc.vector.tensor_reduce(out=mx[:], in_=bank[:].rearrange("p h m -> p m h"), axis=AX.X, op=ALU.max)
+            nc.vector.tensor_tensor(out=e_last[:, :, j, :], in0=bank[:], in1=mx[:].unsqueeze(1).to_broadcast([P, H, P]),
+                                    op=ALU.subtract)
+            nc.scalar.activation(out=e_last[:, :, j, :], in_=e_last[:, :, j, :], func=ACT.Exp, scale=1.0 / 32.0)
+            for h in range(H):
+                nc.tensor.matmul(out=sum_bank[:, j, :], lhsT=ident[:], rhs=e_last[:, h, j, :], start=(h == 0), stop=(h == H - 1))
+        n, members = inv_at[UNITS]
+        invert(n, len(members))
+        nc.scalar.activation(out=roots_last[:], in_=sum_bank[:], func=ACT.Abs_reciprocal_sqrt)
+        nc.scalar.activation(out=rinv_last[:], in_=roots_last[:], func=ACT.Square)
+        for c in range(len(members)):
+            scale_block(members[c][0], members[c][1], nc.vector if c < 2 else nc.gpsimd)
+        for h in range(H):
+            nc.vector.tensor_tensor(out=e_last[:, h], in0=e_last[:, h], in1=rinv_last[:], op=ALU.mult)
+            nc.scalar.dma_start(out=out_row[h], in_=e_last[:, h].rearrange("p j m -> p (j m)"))

@@ -21,7 +21,7 @@ NCH = 4
 UNITS = 2 * NCH * H
 W_BUFS = 10
 AHEAD = 4
-ROWS = ()
+ROWS = tuple(range(16, 30, 2))
 TURN_LAG = 2
 EXP_LAG = 1
 BATCHES = ((9, 22, 24), (23, 29, 31), (30, 31, 32))

@@ -21,7 +21,7 @@ NCH = 4
 UNITS = 2 * NCH * H
 W_BUFS = 10
 AHEAD = 4
-ROWS = tuple(range(16, 30, 2))
+ROWS = tuple(range(8, 30, 4))
 TURN_LAG = 2
 EXP_LAG = 1
 BATCHES = ((9, 22, 24), (23, 29, 31), (30, 31, 32))
@@ -37,9 +37,7 @@ def tile_selfattention_pa_kernel(tc, tokens, Wq, bq, Wk, bk, out):
         wraw_pool = ctx.enter_context(tc.tile_pool(name="wraw", bufs=W_BUFS))
         stage = ctx.enter_context(tc.tile_pool(name="stage", bufs=3))
         soft = ctx.enter_context(tc.tile_pool(name="soft", bufs=2))
-        ps_t = ctx.enter_context(tc.psum_pool(name="ps_t", bufs=4))
-        ps_m = ctx.enter_context(tc.psum_pool(name="ps_m", bufs=3))
-        ps_s = ctx.enter_context(tc.psum_pool(name="ps_s", bufs=1))
+        ps_m = ctx.enter_context(tc.psum_pool(name="ps_m", bufs=8))
         ctx.enter_context(tc.manual_schedule())
 
         w_src = {"k": Wk.rearrange("(i l h e) k -> i h l (e k)", i=NCH, l=P, h=H, e=2),
@@ -104,7 +102,7 @@ def tile_selfattention_pa_kernel(tc, tokens, Wq, bq, Wk, bk, out):
             if u % 2 == 0:
                 wt_grp[u // 2] = stage.tile([P, 2, 2, 4 * 2 * P], BF16, name="wt_grp", align_bytes=64)
             for g in range(2):
-                bank = ps_t.tile([P, 4 * P], F32, name="bank_t")
+                bank = ps_m.tile([P, 4 * P], F32, name="bank_m")
                 for e in range(2):
                     for v in range(2):
                         nc.tensor.transpose(out=bank[:, (2 * e + v) * P:(2 * e + v + 1) * P],
@@ -163,7 +161,7 @@ def tile_selfattention_pa_kernel(tc, tokens, Wq, bq, Wk, bk, out):
 
         def turn(u):
             words = rows[u][:].rearrange("l e v p b -> l e v (p b)").bitcast(F32)
-            bank = ps_t.tile([P, 4 * P], F32, name="bank_t")
+            bank = ps_m.tile([P, 4 * P], F32, name="bank_m")
             for v in range(2):
                 for e in range(2):
                     nc.tensor.transpose(out=bank[:, (2 * v + e) * P:(2 * v + e + 1) * P], in_=words[:, e, v, :],
@@ -171,10 +169,10 @@ def tile_selfattention_pa_kernel(tc, tokens, Wq, bq, Wk, bk, out):
             nc.scalar.copy(out=qk_grp[u // 2][:, u % 2].rearrange("p a l e b -> p a l (e b)").bitcast(F32),
                            in_=bank[:].rearrange("p (v e l) -> p v l e", v=2, e=2))
 
-        def add_bias(u):
+        def add_bias(u, banks=(0, 1)):
             which, i, h = unit(u)
             b_v = bias[which][:].rearrange("p (i l h e) -> p i h l e", i=NCH, l=P, h=H, e=2)[:, i, h]
-            for a in range(2):
+            for a in banks:
                 nc.vector.tensor_tensor(out=qk_grp[u // 2][:, u % 2, a],
                                         in0=banks_m[u][a][:].rearrange("p (b e l) -> p l e b", b=2, e=2),
                                         in1=b_v.unsqueeze(3).to_broadcast([P, P, 2, 2]), op=ALU.add)
@@ -193,9 +191,9 @@ def tile_selfattention_pa_kernel(tc, tokens, Wq, bq, Wk, bk, out):
 
         def scores(i, j, pool=None):
             if pool is None:
-                bank_s[i, j] = ps_s.tile([P, H, P], F32, name="bank_s")
+                bank_s[i, j] = ps_m.tile([P, H, P], F32, name="bank_m")
             else:
-                bank_s[i, j] = pool.tile([P, H, P], F32, name="bank_t")
+                bank_s[i, j] = pool.tile([P, H, P], F32, name="bank_m")
             for h in range(H):
                 for a in range(2):
                     nc.tensor.matmul_mx(out=bank_s[i, j][:, h, :],
@@ -203,12 +201,15 @@ def tile_selfattention_pa_kernel(tc, tokens, Wq, bq, Wk, bk, out):
                                         rhs=codes["k"][:, j, h, a, :].bitcast(FP8X4), rhs_scale=scl["k"][:, j, h, a, :],
                                         start=(a == 0), stop=(a == 1))
 
-        def shift(i, j):
-            mx = soft.tile([P, P], F32, name="mx")
-            nc.vector.tensor_reduce(out=mx[:], in_=bank_s[i, j][:].rearrange("p h m -> p m h"), axis=AX.X, op=ALU.max)
-            e_t[i, j] = soft.tile([P, H, P], F32, name="e_t", bufs=12)
-            nc.vector.tensor_tensor(out=e_t[i, j][:], in0=bank_s[i, j][:],
-                                    in1=mx[:].unsqueeze(1).to_broadcast([P, H, P]), op=ALU.subtract)
+        mx = {}
+
+        def largest(i, j):
+            mx[i, j] = soft.tile([P, P], F32, name="mx", bufs=3)
+            nc.vector.tensor_reduce(out=mx[i, j][:], in_=bank_s[i, j][:].rearrange("p h m -> p m h"), axis=AX.X, op=ALU.max)
+
+        def shift(i, j, out):
+            nc.vector.tensor_tensor(out=out, in0=bank_s[i, j][:], in1=mx[i, j][:].unsqueeze(1).to_broadcast([P, H, P]),
+                                    op=ALU.subtract)
 
         def expo(i, j):
             nc.scalar.activation(out=e_t[i, j][:], in_=e_t[i, j][:], func=ACT.Exp, scale=1.0 / 32.0)
@@ -302,10 +303,9 @@ def tile_selfattention_pa_kernel(tc, tokens, Wq, bq, Wk, bk, out):
                 ahead(2)
             elif u == 1:
                 ahead(3)
-                ahead(4)
-                ahead(5)
-            else:
+            elif u % 2 == 0:
                 ahead(u + AHEAD)
+                ahead(u + AHEAD + 1)
             if u - TURN_LAG in ROWS:
                 turn(u - TURN_LAG)
             if u % 2 == 0:
@@ -316,15 +316,24 @@ def tile_selfattention_pa_kernel(tc, tokens, Wq, bq, Wk, bk, out):
                 products(u)
             if u in work:
                 scores(work[u][0], work[u][1])
+            if u == 1:
+                ahead(4)
+                ahead(5)
             if u in ROWS:
                 add_bias_rows(u)
-            else:
-                add_bias(u)
+            if u not in ROWS:
+                add_bias(u, (0,))
             if u in work:
-                shift(work[u][0], work[u][1])
+                largest(work[u][0], work[u][1])
+            if u not in ROWS:
+                add_bias(u, (1,))
+            if u in work:
+                i, j = work[u]
+                e_t[i, j] = soft.tile([P, H, P], F32, name="e_t", bufs=12)
+                shift(i, j, e_t[i, j][:])
             softmax_end(u)
             if u == 3:
-                spread_bias("q", 0, ps_t, "bank_t")
+                spread_bias("q", 0, ps_m, "bank_m")
             if u % 4 == 1 and u // 4 + 2 < 2 * NCH:
                 fetch_bias(unit(u // 4 * 4 + 2 * H)[0], unit(u // 4 * 4 + 2 * H)[1])
             if u == 1:
@@ -342,16 +351,15 @@ def tile_selfattention_pa_kernel(tc, tokens, Wq, bq, Wk, bk, out):
         rinv_last = soft.tile([P, NCH, P], F32, name="rinv_last", bufs=1)
         roots_last = soft.tile([P, NCH, P], F32, name="roots_last", bufs=1)
         for j in range(NCH):
-            scores(NCH - 1, j, ps_t)
+            scores(NCH - 1, j, ps_m)
         sum_bank = ps_m.tile([P, NCH, P], F32, name="bank_m")
         for u in range(UNITS, UNITS + EXP_LAG):
             softmax_end(u)
+        largest(NCH - 1, 0)
         for j in range(NCH):
-            mx = soft.tile([P, P], F32, name="mx")
-            bank = bank_s[NCH - 1, j]
-            nc.vector.tensor_reduce(out=mx[:], in_=bank[:].rearrange("p h m -> p m h"), axis=AX.X, op=ALU.max)
-            nc.vector.tensor_tensor(out=e_last[:, :, j, :], in0=bank[:], in1=mx[:].unsqueeze(1).to_broadcast([P, H, P]),
-                                    op=ALU.subtract)
+            if j + 1 < NCH:
+                largest(NCH - 1, j + 1)
+            shift(NCH - 1, j, e_last[:, :, j, :])
             nc.scalar.activation(out=e_last[:, :, j, :], in_=e_last[:, :, j, :], func=ACT.Exp, scale=1.0 / 32.0)
             for h in range(H):
                 nc.tensor.matmul(out=sum_bank[:, j, :], lhsT=ident[:], rhs=e_last[:, h, j, :], start=(h == 0), stop=(h == H - 1))

from contextlib import ExitStack

import concourse.mybir as mybir
from concourse.masks import make_identity

F32 = mybir.dt.float32
BF16 = mybir.dt.bfloat16
U32 = mybir.dt.uint32
U8 = mybir.dt.uint8
I32 = mybir.dt.int32
FP8X4 = mybir.dt.float8_e4m3fn_x4
ALU = mybir.AluOpType
ACT = mybir.ActivationFunctionType
AX = mybir.AxisListType

P = 128
H = 4
L = 512
D = 1024
NCH = 4
UNITS = 2 * NCH * H
W_BUFS = 10
AHEAD = 4
ROWS = tuple(range(8, 30, 4))
TURN_LAG = 2
EXP_LAG = 1
BATCHES = ((9, 22, 24), (23, 29, 31), (30, 31, 32))
MAXB = 6

FLOPS = 2 * (2 * H * D) * D * L + 2 * H * L * L * D


def tile_selfattention_pa_kernel(tc, tokens, Wq, bq, Wk, bk, out):
    nc = tc.nc
    with ExitStack() as ctx:
        const = ctx.enter_context(tc.tile_pool(name="const", bufs=1))
        wraw_pool = ctx.enter_context(tc.tile_pool(name="wraw", bufs=W_BUFS))
        stage = ctx.enter_context(tc.tile_pool(name="stage", bufs=3))
        soft = ctx.enter_context(tc.tile_pool(name="soft", bufs=2))
        ps_m = ctx.enter_context(tc.psum_pool(name="ps_m", bufs=8))
        ctx.enter_context(tc.manual_schedule())

        w_src = {"k": Wk.rearrange("(i l h e) k -> i h l (e k)", i=NCH, l=P, h=H, e=2),
                 "q": Wq.rearrange("(i l h e) k -> i h l (e k)", i=NCH, l=P, h=H, e=2)}
        out_row = out[:, L - P:L, :]
        out_v = out.rearrange("h (i p) (j m) -> i j p h m", p=P, m=P)

        def unit(u):
            return ("k" if (u // H) % 2 == 0 else "q"), u // (2 * H), u % H

        tok_raw = const.tile([P, 2, 4, L], BF16, name="tok_raw")
        tok_grp = const.tile([P, 2, L, 4], BF16, name="tok_grp", align_bytes=64)
        tok_codes = const.tile([P, 2, L], U32, name="tok_codes", align_bytes=64)
        tok_scl = const.tile([P, 2, L], U8, name="tok_scl", align_bytes=64)
        bias = {"k": const.tile([P, H * D], BF16, name="bias_k"), "q": const.tile([P, H * D], BF16, name="bias_q")}
        bias_col = {"k": const.tile([P, NCH, 2 * H], BF16, name="bias_col_k"),
                    "q": const.tile([P, NCH, 2 * H], BF16, name="bias_col_q")}
        codes = {"k": const.tile([P, NCH, H, 2, P], U32, name="k_codes", align_bytes=64),
                 "q": const.tile([P, NCH, H, 2, P], U32, name="q_codes", align_bytes=64)}
        scl = {"k": const.tile([P, NCH, H, 2, P], U8, name="k_scl", align_bytes=64),
               "q": const.tile([P, NCH, H, 2, P], U8, name="q_scl", align_bytes=64)}

        b_rows = const.tile([P, 2 * P], BF16, name="b_rows")
        nc.vector.memset(b_rows[32:64, :].bitcast(I32), 0)
        nc.vector.memset(b_rows[64:128, :].bitcast(I32), 0)
        nc.scalar.dma_start(out=b_rows[0:16, :], in_=bk.rearrange("(r n) -> r n", n=2 * P))
        nc.scalar.dma_start(out=b_rows[16:32, :], in_=bq.rearrange("(r n) -> r n", n=2 * P))
        ident = const.tile([P, P], F32, name="ident")
        make_identity(nc, ident[:])
        ident_b = const.tile([P, P], BF16, name="ident_b")
        make_identity(nc, ident_b[:])

        w_raw = {}
        wt_grp = {}
        w_codes = {}
        w_scl = {}
        qk_grp = {}
        banks_m = {}
        rows = {}

        def load(u):
            which, i, h = unit(u)
            w_raw[u] = wraw_pool.tile([P, 2, D], BF16, name="w_raw")
            nc.sync.dma_start(out=w_raw[u][:].rearrange("p e k -> p (e k)"), in_=w_src[which][i, h])

        def fetch_bias(which, i):
            src = bk if which == "k" else bq
            nc.scalar.dma_start(out=bias[which][:, 2 * H * P * i:2 * H * P * (i + 1)],
                                in_=src[2 * H * P * i:2 * H * P * (i + 1)].partition_broadcast(P))

        def spread_bias(which, i, pool, name):
            for half in range(2):
                bank = pool.tile([P, 4 * P], F32, name=name)
                for z in range(2):
                    r = (0 if which == "k" else 16) + 4 * i + 2 * half + z
                    nc.tensor.matmul(out=bank[:, 2 * P * z:2 * P * (z + 1)], lhsT=ident_b[:, r:r + 1].to_broadcast([P, P]),
                                     rhs=b_rows[:], start=True, stop=True)
                nc.scalar.copy(out=bias[which][:, 4 * P * (2 * i + half):4 * P * (2 * i + half + 1)], in_=bank[:])

        def transposes(u):
            w32 = w_raw[u][:].bitcast(F32)
            if u % 2 == 0:
                wt_grp[u // 2] = stage.tile([P, 2, 2, 4 * 2 * P], BF16, name="wt_grp", align_bytes=64)
            for g in range(2):
                bank = ps_m.tile([P, 4 * P], F32, name="bank_m")
                for e in range(2):
                    for v in range(2):
                        nc.tensor.transpose(out=bank[:, (2 * e + v) * P:(2 * e + v + 1) * P],
                                            in_=w32[:, e, 256 * g + P * v:256 * g + P * (v + 1)], identity=ident[:])
                nc.scalar.copy(out=wt_grp[u // 2][:, u % 2, g, :].bitcast(F32).rearrange("p (e l v) -> p e l v", e=2, v=2),
                               in_=bank[:].rearrange("p (e v l) -> p e l v", e=2, v=2))

        def quant_w(t):
            w_codes[t] = stage.tile([P, 2, 2, 2 * P], U32, name="w_codes", align_bytes=64)
            w_scl[t] = stage.tile([P, 2, 2, 2 * P], U8, name="w_scl", align_bytes=64)
            nc.vector.quantize_mx(out=w_codes[t][:].rearrange("p x g c -> p (x g c)").bitcast(FP8X4),
                                  scales=w_scl[t][:].rearrange("p x g c -> p (x g c)"),
                                  in_=wt_grp[t][:].rearrange("p x g c -> p (x g c)"))

        def quant_w_half(t, x):
            if x == 0:
                w_codes[t] = stage.tile([P, 2, 2, 2 * P], U32, name="w_codes", align_bytes=64)
                w_scl[t] = stage.tile([P, 2, 2, 2 * P], U8, name="w_scl", align_bytes=64)
            nc.vector.quantize_mx(out=w_codes[t][:, x].rearrange("p g c -> p (g c)").bitcast(FP8X4),
                                  scales=w_scl[t][:, x].rearrange("p g c -> p (g c)"),
                                  in_=wt_grp[t][:, x].rearrange("p g c -> p (g c)"))

        def products(u):
            banks_m[u] = []
            for a in range(2):
                bank = ps_m.tile([P, 4 * P], F32, name="bank_m")
                banks_m[u].append(bank)
                for b in range(2):
                    cb = 2 * a + b
                    for g in range(2):
                        nc.tensor.matmul_mx(out=bank[:, 2 * P * b:2 * P * (b + 1)],
                                            lhsT=tok_codes[:, g, P * cb:P * (cb + 1)].bitcast(FP8X4),
                                            lhsT_scale=tok_scl[:, g, P * cb:P * (cb + 1)],
                                            rhs=w_codes[u // 2][:, u % 2, g, :].bitcast(FP8X4),
                                            rhs_scale=w_scl[u // 2][:, u % 2, g, :],
                                            start=(g == 0), stop=(g == 1))

        def products_rows(u):
            banks_m[u] = []
            for e in range(2):
                bank = ps_m.tile([P, 4 * P], F32, name="bank_m")
                banks_m[u].append(bank)
                for g in range(2):
                    nc.tensor.matmul_mx(out=bank[:],
                                        lhsT=w_codes[u // 2][:, u % 2, g, P * e:P * (e + 1)].bitcast(FP8X4),
                                        lhsT_scale=w_scl[u // 2][:, u % 2, g, P * e:P * (e + 1)],
                                        rhs=tok_codes[:, g, :].bitcast(FP8X4), rhs_scale=tok_scl[:, g, :],
                                        start=(g == 0), stop=(g == 1))

        def add_bias_rows(u):
            which, i, h = unit(u)
            rows[u] = stage.tile([P, 2, 2, P, 2], BF16, name="rows", align_bytes=64)
            for e in range(2):
                nc.scalar.activation(out=rows[u][:, e], in_=banks_m[u][e][:].rearrange("l (v b p) -> l v p b", v=2, b=2),
                                     func=ACT.Identity, bias=bias_col[which][:, i, 2 * h + e:2 * h + e + 1])

        def turn(u):
            words = rows[u][:].rearrange("l e v p b -> l e v (p b)").bitcast(F32)
            bank = ps_m.tile([P, 4 * P], F32, name="bank_m")
            for v in range(2):
                for e in range(2):
                    nc.tensor.transpose(out=bank[:, (2 * v + e) * P:(2 * v + e + 1) * P], in_=words[:, e, v, :],
                                        identity=ident[:])
            nc.scalar.copy(out=qk_grp[u // 2][:, u % 2].rearrange("p a l e b -> p a l (e b)").bitcast(F32),
                           in_=bank[:].rearrange("p (v e l) -> p v l e", v=2, e=2))

        def add_bias(u, banks=(0, 1)):
            which, i, h = unit(u)
            b_v = bias[which][:].rearrange("p (i l h e) -> p i h l e", i=NCH, l=P, h=H, e=2)[:, i, h]
            for a in banks:
                nc.vector.tensor_tensor(out=qk_grp[u // 2][:, u % 2, a],
                                        in0=banks_m[u][a][:].rearrange("p (b e l) -> p l e b", b=2, e=2),
                                        in1=b_v.unsqueeze(3).to_broadcast([P, P, 2, 2]), op=ALU.add)

        def quant_qk(t):
            which, i, h = unit(2 * t)
            nc.vector.quantize_mx(out=codes[which][:, i, h:h + 2].rearrange("p x a l -> p (x a l)").bitcast(FP8X4),
                                  scales=scl[which][:, i, h:h + 2].rearrange("p x a l -> p (x a l)"),
                                  in_=qk_grp[t][:].rearrange("p x a l e b -> p (x a l e b)"))

        bank_s = {}
        e_t = {}
        sums = {}
        rinv = {}
        place = {}

        def scores(i, j, pool=None):
            if pool is None:
                bank_s[i, j] = ps_m.tile([P, H, P], F32, name="bank_m")
            else:
                bank_s[i, j] = pool.tile([P, H, P], F32, name="bank_m")
            for h in range(H):
                for a in range(2):
                    nc.tensor.matmul_mx(out=bank_s[i, j][:, h, :],
                                        lhsT=codes["q"][:, i, h, a, :].bitcast(FP8X4), lhsT_scale=scl["q"][:, i, h, a, :],
                                        rhs=codes["k"][:, j, h, a, :].bitcast(FP8X4), rhs_scale=scl["k"][:, j, h, a, :],
                                        start=(a == 0), stop=(a == 1))

        mx = {}

        def largest(i, j):
            mx[i, j] = soft.tile([P, P], F32, name="mx", bufs=3)
            nc.vector.tensor_reduce(out=mx[i, j][:], in_=bank_s[i, j][:].rearrange("p h m -> p m h"), axis=AX.X, op=ALU.max)

        def shift(i, j, out):
            nc.vector.tensor_tensor(out=out, in0=bank_s[i, j][:], in1=mx[i, j][:].unsqueeze(1).to_broadcast([P, H, P]),
                                    op=ALU.subtract)

        def expo(i, j):
            nc.scalar.activation(out=e_t[i, j][:], in_=e_t[i, j][:], func=ACT.Exp, scale=1.0 / 32.0)

        def total(i, j):
            n, c = place[i, j]
            if c == 0:
                sums[n] = soft.tile([P, MAXB, P], F32, name="sums")
            half = soft.tile([P, 2, P], F32, name="half")
            nc.gpsimd.tensor_tensor(out=half[:], in0=e_t[i, j][:, 0:2, :], in1=e_t[i, j][:, 2:4, :], op=ALU.add)
            whole = soft.tile([P, P], F32, name="whole")
            nc.gpsimd.tensor_tensor(out=whole[:], in0=half[:, 0, :], in1=half[:, 1, :], op=ALU.add)
            nc.gpsimd.tensor_tensor(out=sums[n][:, c, :], in0=whole[:], in1=whole[:], op=ALU.mult)

        def invert(n, size):
            rinv[n] = soft.tile([P, MAXB, P], F32, name="rinv")
            nc.scalar.activation(out=rinv[n][:, 0:size, :], in_=sums[n][:, 0:size, :], func=ACT.Abs_reciprocal_sqrt)

        def scale_block(i, j, eng):
            n, c = place[i, j]
            eng.tensor_tensor(out=e_t[i, j][:], in0=e_t[i, j][:],
                              in1=rinv[n][:, c, :].unsqueeze(1).to_broadcast([P, H, P]), op=ALU.mult)
            nc.sync.dma_start(out=out_v[i, j], in_=e_t[i, j][:])

        tok_src = tokens.rearrange("(g v p e) c -> g p v (e c)", g=2, v=2, p=P, e=2)
        def load_tokens(g):
            nc.sync.dma_start(out=tok_raw[:, g].rearrange("p (v e) c -> p v (e c)", v=2), in_=tok_src[g])

        def token_half(z):
            cols = slice(L // 2 * z, L // 2 * (z + 1))
            for g in range(2):
                nc.vector.tensor_copy(out=tok_grp[:, g, cols].rearrange("p (c i) t -> p c t i", i=4),
                                      in_=tok_raw[:, g, :, cols].rearrange("p t (c i) -> p c t i", i=4))
            for g in range(2):
                nc.vector.quantize_mx(out=tok_codes[:, g, cols].bitcast(FP8X4), scales=tok_scl[:, g, cols],
                                      in_=tok_grp[:, g, cols].rearrange("p c t -> p (c t)"))

        for z in range(1):
            load(z)
        load_tokens(0)
        load_tokens(1)
        for u in range(1, W_BUFS):
            load(u)
            if u == 2 and len(ROWS) > 0:
                for which, b in (("k", bk), ("q", bq)):
                    nc.sync.dma_start(out=bias_col[which][:], in_=b.rearrange("(i l n) -> l i n", i=NCH, l=P))

        def ahead(u):
            if u < UNITS:
                transposes(u)
                if u + W_BUFS < UNITS:
                    load(u + W_BUFS)

        work = {}
        for c in range(1, 2 * NCH - 1):
            done = [(c // 2, j) for j in range(c // 2 + 1)] if c % 2 == 1 else [(i, c // 2) for i in range(c // 2)]
            for n in range(len(done)):
                work[H * (c + 1) + 1 + n] = done[n]
        inv_at = {}
        for n in range(len(BATCHES)):
            first, end, at = BATCHES[n]
            members = [work[u] for u in range(first, end + 1) if u in work]
            for c in range(len(members)):
                place[members[c]] = (n, c)
            inv_at[at] = (n, members)

        def softmax_end(u):
            if u - EXP_LAG in work:
                expo(work[u - EXP_LAG][0], work[u - EXP_LAG][1])
                total(work[u - EXP_LAG][0], work[u - EXP_LAG][1])
            if u in inv_at and u < UNITS:
                n, members = inv_at[u]
                invert(n, len(members))
                for b in members:
                    scale_block(b[0], b[1], nc.gpsimd)

        ready = {}
        for t in range(UNITS // 2):
            at = max(u + TURN_LAG if u in ROWS else u for u in (2 * t, 2 * t + 1))
            ready.setdefault(at, []).append(t)

        ahead(0)
        token_half(0)
        quant_w_half(0, 0)
        spread_bias("k", 0, ps_m, "bank_m")
        ahead(1)
        token_half(1)
        quant_w_half(0, 1)
        for u in range(UNITS):
            if u == 0:
                ahead(2)
            elif u == 1:
                ahead(3)
            elif u % 2 == 0:
                ahead(u + AHEAD)
                ahead(u + AHEAD + 1)
            if u - TURN_LAG in ROWS:
                turn(u - TURN_LAG)
            if u % 2 == 0:
                qk_grp[u // 2] = stage.tile([P, 2, 2, P, 2, 2], BF16, name="qk_grp", bufs=4, align_bytes=64)
            if u in ROWS:
                products_rows(u)
            else:
                products(u)
            if u in work:
                scores(work[u][0], work[u][1])
            if u == 1:
                ahead(4)
                ahead(5)
            if u in ROWS:
                add_bias_rows(u)
            if u not in ROWS:
                add_bias(u, (0,))
            if u in work:
                largest(work[u][0], work[u][1])
            if u not in ROWS:
                add_bias(u, (1,))
            if u in work:
                i, j = work[u]
                e_t[i, j] = soft.tile([P, H, P], F32, name="e_t", bufs=12)
                shift(i, j, e_t[i, j][:])
            softmax_end(u)
            if u == 3:
                spread_bias("q", 0, ps_m, "bank_m")
            if u % 4 == 1 and u // 4 + 2 < 2 * NCH:
                fetch_bias(unit(u // 4 * 4 + 2 * H)[0], unit(u // 4 * 4 + 2 * H)[1])
            if u == 1:
                quant_w(1)
            if u % 2 == 1 and u + AHEAD < UNITS:
                quant_w(u // 2 + AHEAD // 2)
            for t in ready.get(u, []):
                quant_qk(t)
        for u in range(UNITS, UNITS + TURN_LAG):
            if u - TURN_LAG in ROWS:
                turn(u - TURN_LAG)
            for t in ready.get(u, []):
                quant_qk(t)
        e_last = soft.tile([P, H, NCH, P], F32, name="e_last", bufs=1)
        rinv_last = soft.tile([P, NCH, P], F32, name="rinv_last", bufs=1)
        roots_last = soft.tile([P, NCH, P], F32, name="roots_last", bufs=1)
        for j in range(NCH):
            scores(NCH - 1, j, ps_m)
        sum_bank = ps_m.tile([P, NCH, P], F32, name="bank_m")
        for u in range(UNITS, UNITS + EXP_LAG):
            softmax_end(u)
        largest(NCH - 1, 0)
        for j in range(NCH):
            if j + 1 < NCH:
                largest(NCH - 1, j + 1)
            shift(NCH - 1, j, e_last[:, :, j, :])
            nc.scalar.activation(out=e_last[:, :, j, :], in_=e_last[:, :, j, :], func=ACT.Exp, scale=1.0 / 32.0)
            for h in range(H):
                nc.tensor.matmul(out=sum_bank[:, j, :], lhsT=ident[:], rhs=e_last[:, h, j, :], start=(h == 0), stop=(h == H - 1))
        n, members = inv_at[UNITS]
        invert(n, len(members))
        nc.scalar.activation(out=roots_last[:], in_=sum_bank[:], func=ACT.Abs_reciprocal_sqrt)
        nc.scalar.activation(out=rinv_last[:], in_=roots_last[:], func=ACT.Square)
        for c in range(len(members)):
            scale_block(members[c][0], members[c][1], nc.vector if c < 2 else nc.gpsimd)
        for h in range(H):
            nc.vector.tensor_tensor(out=e_last[:, h], in0=e_last[:, h], in1=rinv_last[:], op=ALU.mult)
            nc.scalar.dma_start(out=out_row[h], in_=e_last[:, h].rearrange("p j m -> p (j m)"))
